import numpy as np
import ml_dtypes


def mxq(x, axis, fmt="e4m3"):
    dtype, down = {"e4m3": (ml_dtypes.float8_e4m3fn, 7), "e5m2": (ml_dtypes.float8_e5m2, 14)}[fmt]
    v = np.moveaxis(np.asarray(x, np.float32).astype(ml_dtypes.bfloat16).astype(np.float64), axis, -1)
    blocks = v.reshape(v.shape[:-1] + (-1, 32))
    amax = np.abs(blocks).max(-1, keepdims=True)
    byte = np.maximum(np.where(amax > 0, np.frexp(amax)[1] - 1 + 127, 0) - down, 1)
    scale = np.exp2(byte - 127.0)
    codes = (blocks / scale).astype(np.float32).astype(dtype).astype(np.float64)
    return np.moveaxis((codes * scale).reshape(v.shape), -1, axis)


WIDE = False


def mx_kscale(k):
    if not WIDE:
        return np.ones(k)
    levels = np.array([10, -10, 5, -5, 0])
    if k % 512:
        return np.exp2(np.random.permutation(np.resize(levels, k // 32))).repeat(32)
    a = np.empty((k // 512, 16))
    for p in range(k // 512):
        a[p, :8] = np.random.permutation(np.resize(levels, 8))
        for g in range(8):
            far = levels[np.abs(levels - a[p, g]) >= 10]
            a[p, g + 8] = far[np.random.randint(len(far))]
    return np.exp2(a.ravel()).repeat(32)


BF16 = ml_dtypes.bfloat16


def bf(x):
    return np.asarray(x, np.float32).astype(BF16)


def f64(x):
    return np.asarray(x).astype(np.float64)


B, T, D, H, DH, F = 4, 256, 1024, 16, 64, 4096
A = H * DH
EPS = 1e-6


def layer_norm(v, gain, bias):
    mu = v.mean(-1, keepdims=True)
    var = np.square(v - mu).mean(-1, keepdims=True)
    return (v - mu) * (1.0 / np.sqrt(var + EPS)) * gain + bias


def setup_inputs():
    s = mx_kscale(D)
    r = np.random.standard_normal
    return {"x": bf(r((B, T, D))),
            "ln1_gain": bf((1.0 + 0.1 * r(D)) * s),
            "ln1_bias": bf(0.1 * r(D) * s),
            "wq": bf(r((D, A)) / np.sqrt(D) / s[:, None]),
            "bq": bf(0.1 * r(A)),
            "wk": bf(r((D, A)) / np.sqrt(D) / s[:, None]),
            "bk": bf(0.1 * r(A)),
            "wv": bf(r((D, A)) / np.sqrt(D) / s[:, None]),
            "bv": bf(0.1 * r(A))}


def reference(x, ln1_gain, ln1_bias, wq, bq, wk, bk, wv, bv):
    h = layer_norm(f64(x), f64(ln1_gain), f64(ln1_bias))
    hq = mxq(h, 2, "e4m3")
    q = ((hq @ mxq(f64(wq), 0, "e4m3")) + f64(bq)).reshape(B, T, H, DH)
    k = ((hq @ mxq(f64(wk), 0, "e4m3")) + f64(bk)).reshape(B, T, H, DH)
    v = ((hq @ mxq(f64(wv), 0, "e4m3")) + f64(bv)).reshape(B, T, H, DH)
    return q, k, v

@@ -1,0 +1,259 @@
+from contextlib import ExitStack
+
+import concourse.mybir as mybir
+from concourse.masks import make_identity
+
+F32 = mybir.dt.float32
+BF16 = mybir.dt.bfloat16
+U32 = mybir.dt.uint32
+U8 = mybir.dt.uint8
+FP8X4 = mybir.dt.float8_e4m3fn_x4
+ALU = mybir.AluOpType
+ACT = mybir.ActivationFunctionType
+
+P = 128
+PACK = 4
+K_PASS = P * PACK
+D = 1024
+PASSES = D // K_PASS
+CHUNKS = D // P
+TOKENS = 1024
+TOKEN_TILES = TOKENS // P
+HALF_TILES = TOKEN_TILES // 2
+HALF_TOKENS = HALF_TILES * P
+WIDTH = 1024
+N_BLOCK = 512
+BLOCKS_PER_WEIGHT = WIDTH // N_BLOCK
+BLOCKS = 3 * BLOCKS_PER_WEIGHT
+STAT_PIECE = 512
+RUN = 4
+EPS = 1e-6
+SCALAR_SHARE = 4
+
+FLOPS = 2 * TOKENS * D * 3 * WIDTH
+
+
+def regroup(copy, grouped, rows):
+    copy(
+        out=grouped.rearrange("p (c i) t -> p c t i", i=RUN),
+        in_=rows.rearrange("p t (c i) -> p c t i", i=RUN),
+    )
+
+
+def tile_swidtblock_pa_kernel(
+    tc, x, ln1_gain, ln1_bias, wq, bq, wk, bk, wv, bv, out_0, out_1, out_2
+):
+    nc = tc.nc
+    x_rows = x.flatten_outer_dims()
+    weights = [wq, wk, wv]
+    biases = [bq, bk, bv]
+    outs = [o.rearrange("b t h e -> (b t) (h e)") for o in (out_0, out_1, out_2)]
+
+    with ExitStack() as ctx:
+        keep = ctx.enter_context(tc.tile_pool(name="keep", bufs=1))
+        h_stage = ctx.enter_context(tc.tile_pool(name="h_stage", bufs=2))
+        w_stage = ctx.enter_context(tc.tile_pool(name="w_stage", bufs=4))
+        o_stage = ctx.enter_context(tc.tile_pool(name="o_stage", bufs=8))
+        psum = ctx.enter_context(tc.psum_pool(name="psum", bufs=4))
+
+        ident_f32 = keep.tile([P, P], F32)
+        make_identity(nc, ident_f32[:])
+        ident_bf = keep.tile([P, P], BF16)
+        nc.vector.tensor_copy(out=ident_bf[:], in_=ident_f32[:])
+        eps_t = keep.tile([P, 1], F32)
+        nc.vector.memset(eps_t[:], EPS)
+        warm = keep.tile([P, 1], F32)
+        nc.scalar.activation(out=warm[:], in_=eps_t[:], func=ACT.Sqrt)
+
+        gain_bf = keep.tile([P, PASSES, PACK], BF16)
+        lnb_bf = keep.tile([P, PASSES, PACK], BF16)
+        with nc.allow_non_contiguous_dma(reason="four neighbouring values a partition"):
+            nc.scalar.dma_start(
+                out=gain_bf[:], in_=ln1_gain.rearrange("(g p t) -> p g t", p=P, t=PACK)
+            )
+            nc.scalar.dma_start(
+                out=lnb_bf[:], in_=ln1_bias.rearrange("(g p t) -> p g t", p=P, t=PACK)
+            )
+        norm_cols = keep.tile([P, 2 * CHUNKS], F32)
+        nc.vector.tensor_copy(
+            out=norm_cols[:, 0:CHUNKS], in_=gain_bf[:].rearrange("p g t -> p (g t)")
+        )
+        nc.vector.tensor_copy(
+            out=norm_cols[:, CHUNKS : 2 * CHUNKS], in_=lnb_bf[:].rearrange("p g t -> p (g t)")
+        )
+        bias_rows = keep.tile([P, N_BLOCK], BF16)
+        nc.vector.memset(bias_rows[:], 0.0)
+        for w in range(3):
+            nc.scalar.dma_start(
+                out=bias_rows[BLOCKS_PER_WEIGHT * w : BLOCKS_PER_WEIGHT * (w + 1), :],
+                in_=biases[w].rearrange("(r c) -> r c", c=N_BLOCK),
+            )
+
+        x_sb = keep.tile([P, TOKEN_TILES, D], BF16)
+        w_raw = keep.tile([P, 3, PASSES, PACK, WIDTH], BF16)
+
+        def load_x(i):
+            nc.sync.dma_start(out=x_sb[:, i, :], in_=x_rows[P * i : P * (i + 1), :])
+
+        def load_w(w, g):
+            view = weights[w].rearrange("(g p t) n -> g p t n", t=PACK, p=P)
+            nc.sync.dma_start(out=w_raw[:, w, g, :, :], in_=view[g])
+
+        for i in range(HALF_TILES):
+            load_x(i)
+        load_w(0, 0)
+        for i in range(HALF_TILES, TOKEN_TILES):
+            load_x(i)
+        load_w(0, 1)
+        for w in range(1, 3):
+            for g in range(PASSES):
+                load_w(w, g)
+
+        bias_all = keep.tile([P, BLOCKS * N_BLOCK], F32)
+        for b in range(BLOCKS):
+            bias_ps = psum.tile([P, N_BLOCK], F32, tag="acc")
+            nc.tensor.matmul(
+                out=bias_ps[:],
+                lhsT=ident_bf[:, b : b + 1].to_broadcast([P, P]),
+                rhs=bias_rows[:],
+                start=True,
+                stop=True,
+            )
+            nc.scalar.copy(out=bias_all[:, N_BLOCK * b : N_BLOCK * (b + 1)], in_=bias_ps[:])
+
+        stats = keep.tile([P, TOKEN_TILES, D // STAT_PIECE, 6], F32)
+        mean_var = keep.tile([P, TOKEN_TILES, 2], F32)
+        std = keep.tile([P, TOKEN_TILES], F32)
+        rstd = keep.tile([P, TOKEN_TILES], F32)
+        shift = keep.tile([P, TOKEN_TILES], F32)
+        normed = keep.tile([P, TOKEN_TILES, D], F32)
+
+        def normalise(i):
+            for c in range(D // STAT_PIECE):
+                nc.vector.bn_stats(
+                    out=stats[:, i, c, :], in_=x_sb[:, i, STAT_PIECE * c : STAT_PIECE * (c + 1)]
+                )
+            nc.vector.bn_aggr(
+                out=mean_var[:, i, :], in_=stats[:, i, :, :].rearrange("p c s -> p (c s)")
+            )
+            nc.scalar.activation(
+                out=std[:, i : i + 1], in_=mean_var[:, i, 1:2], func=ACT.Sqrt, bias=eps_t[:, 0:1]
+            )
+            nc.vector.reciprocal(out=rstd[:, i : i + 1], in_=std[:, i : i + 1])
+            nc.vector.tensor_scalar(
+                out=shift[:, i : i + 1],
+                in0=mean_var[:, i, 0:1],
+                scalar1=rstd[:, i : i + 1],
+                scalar2=-1.0,
+                op0=ALU.mult,
+                op1=ALU.mult,
+            )
+            nc.gpsimd.tensor_scalar(
+                out=normed[:, i, :].rearrange("p (g t q) -> p g t q", t=PACK, q=P),
+                in0=x_sb[:, i, :].rearrange("p (g q t) -> p g t q", t=PACK, q=P),
+                scalar1=rstd[:, i : i + 1],
+                scalar2=shift[:, i : i + 1],
+                op0=ALU.mult,
+                op1=ALU.add,
+            )
+
+        h_rows = keep.tile([P, 2, CHUNKS, HALF_TOKENS], BF16)
+        h_codes = keep.tile([P, PASSES, TOKENS], U32, align_bytes=64)
+        h_scales = keep.tile([P, PASSES, TOKENS], U8, align_bytes=64)
+
+        def transpose_and_scale(half):
+            for j in range(CHUNKS):
+                turned = psum.tile([P, HALF_TOKENS], F32, tag="turned")
+                for s in range(HALF_TILES):
+                    nc.tensor.transpose(
+                        turned[:, P * s : P * (s + 1)],
+                        normed[:, HALF_TILES * half + s, P * j : P * (j + 1)],
+                        ident_f32[:],
+                    )
+                nc.scalar.activation(
+                    out=h_rows[:, half, j, :],
+                    in_=turned[:],
+                    func=ACT.Identity,
+                    bias=norm_cols[:, CHUNKS + j : CHUNKS + j + 1],
+                    scale=norm_cols[:, j : j + 1],
+                )
+
+        def quantise_h(half):
+            tokens = slice(HALF_TOKENS * half, HALF_TOKENS * (half + 1))
+            for g in range(PASSES):
+                grouped_h = h_stage.tile([P, HALF_TOKENS, PACK], BF16, align_bytes=64)
+                regroup(nc.vector.tensor_copy, grouped_h[:], h_rows[:, half, PACK * g : PACK * (g + 1), :])
+                nc.vector.quantize_mx(
+                    out=h_codes[:, g, tokens].bitcast(FP8X4),
+                    scales=h_scales[:, g, tokens],
+                    in_=grouped_h[:].rearrange("p r t -> p (r t)"),
+                )
+
+        w_codes = keep.tile([P, PASSES, BLOCKS * N_BLOCK], U32, align_bytes=64)
+        w_scales = keep.tile([P, PASSES, BLOCKS * N_BLOCK], U8, align_bytes=64)
+
+        def regroup_w(b, g):
+            w, part = divmod(b, BLOCKS_PER_WEIGHT)
+            grouped_w = w_stage.tile([P, N_BLOCK, PACK], BF16, align_bytes=64)
+            regroup(
+                nc.scalar.copy, grouped_w[:], w_raw[:, w, g, :, N_BLOCK * part : N_BLOCK * (part + 1)]
+            )
+            return grouped_w
+
+        def quantise_w(b, g, grouped_w):
+            cols = slice(N_BLOCK * b, N_BLOCK * (b + 1))
+            nc.vector.quantize_mx(
+                out=w_codes[:, g, cols].bitcast(FP8X4),
+                scales=w_scales[:, g, cols],
+                in_=grouped_w[:].rearrange("p c t -> p (c t)"),
+            )
+
+        def project(b, i):
+            w, part = divmod(b, BLOCKS_PER_WEIGHT)
+            cols = slice(N_BLOCK * b, N_BLOCK * (b + 1))
+            tokens = slice(P * i, P * (i + 1))
+            acc = psum.tile([P, N_BLOCK], F32, tag="acc")
+            for g in range(PASSES):
+                nc.tensor.matmul_mx(
+                    out=acc[:],
+                    lhsT=h_codes[:, g, tokens].bitcast(FP8X4),
+                    lhsT_scale=h_scales[:, g, tokens],
+                    rhs=w_codes[:, g, cols].bitcast(FP8X4),
+                    rhs_scale=w_scales[:, g, cols],
+                    start=(g == 0),
+                    stop=(g == PASSES - 1),
+                )
+            result = o_stage.tile([P, N_BLOCK], F32)
+            if i % SCALAR_SHARE == SCALAR_SHARE - 1:
+                nc.scalar.copy(out=result[:], in_=acc[:])
+                nc.gpsimd.tensor_tensor(
+                    out=result[:], in0=result[:], in1=bias_all[:, cols], op=ALU.add
+                )
+            else:
+                nc.vector.tensor_tensor(
+                    out=result[:], in0=acc[:], in1=bias_all[:, cols], op=ALU.add
+                )
+            nc.sync.dma_start(
+                out=outs[w][tokens, N_BLOCK * part : N_BLOCK * (part + 1)], in_=result[:]
+            )
+
+        for i in range(HALF_TILES):
+            normalise(i)
+        first_0 = regroup_w(0, 0)
+        for i in range(HALF_TILES, TOKEN_TILES):
+            normalise(i)
+        transpose_and_scale(0)
+        first_1 = regroup_w(0, 1)
+        quantise_h(0)
+        quantise_w(0, 0, first_0)
+        quantise_w(0, 1, first_1)
+        transpose_and_scale(1)
+        quantise_h(1)
+        for b in range(BLOCKS):
+            for g in range(PASSES):
+                if b + 1 < BLOCKS:
+                    grouped_next = regroup_w(b + 1, g)
+                for i in range(HALF_TILES * g, HALF_TILES * (g + 1)):
+                    project(b, i)
+                if b + 1 < BLOCKS:
+                    quantise_w(b + 1, g, grouped_next)

@@ -22,15 +22,15 @@ TOKEN_TILES = TOKENS // P
 HALF_TILES = TOKEN_TILES // 2
 HALF_TOKENS = HALF_TILES * P
 WIDTH = 1024
+WEIGHTS = 3
 N_BLOCK = 512
-BLOCKS_PER_WEIGHT = WIDTH // N_BLOCK
-BLOCKS = 3 * BLOCKS_PER_WEIGHT
+PARTS = WIDTH // N_BLOCK
 STAT_PIECE = 512
 RUN = 4
 EPS = 1e-6
-SCALAR_SHARE = 4
+SCALAR_TILE = 1
 
-FLOPS = 2 * TOKENS * D * 3 * WIDTH
+FLOPS = 2 * TOKENS * D * WEIGHTS * WIDTH
 
 
 def regroup(copy, grouped, rows):
@@ -53,20 +53,27 @@ def tile_swidtblock_pa_kernel(
         keep = ctx.enter_context(tc.tile_pool(name="keep", bufs=1))
         h_stage = ctx.enter_context(tc.tile_pool(name="h_stage", bufs=2))
         w_stage = ctx.enter_context(tc.tile_pool(name="w_stage", bufs=4))
-        o_stage = ctx.enter_context(tc.tile_pool(name="o_stage", bufs=8))
-        psum = ctx.enter_context(tc.psum_pool(name="psum", bufs=4))
+        o_stage = ctx.enter_context(tc.tile_pool(name="o_stage", bufs=12))
+        psum = ctx.enter_context(tc.psum_pool(name="psum", bufs=8))
+        ctx.enter_context(tc.manual_schedule())
 
-        ident_f32 = keep.tile([P, P], F32)
-        make_identity(nc, ident_f32[:])
-        ident_bf = keep.tile([P, P], BF16)
-        nc.vector.tensor_copy(out=ident_bf[:], in_=ident_f32[:])
-        eps_t = keep.tile([P, 1], F32)
-        nc.vector.memset(eps_t[:], EPS)
-        warm = keep.tile([P, 1], F32)
-        nc.scalar.activation(out=warm[:], in_=eps_t[:], func=ACT.Sqrt)
-
+        x_sb = keep.tile([P, TOKEN_TILES, D], BF16)
+        w_raw = keep.tile([P, WEIGHTS, PASSES, PACK, WIDTH], BF16)
         gain_bf = keep.tile([P, PASSES, PACK], BF16)
         lnb_bf = keep.tile([P, PASSES, PACK], BF16)
+        bias_all = keep.tile([P, WEIGHTS, WIDTH], BF16)
+
+        def load_x(first, count):
+            nc.sync.dma_start(
+                out=x_sb[:, first : first + count, :],
+                in_=x_rows[P * first : P * (first + count), :].rearrange("(i p) d -> p i d", p=P),
+            )
+
+        def load_w(w, g):
+            view = weights[w].rearrange("(g p t) n -> g p t n", t=PACK, p=P)
+            nc.sync.dma_start(out=w_raw[:, w, g, :, :], in_=view[g])
+
+        load_x(0, 1)
         with nc.allow_non_contiguous_dma(reason="four neighbouring values a partition"):
             nc.scalar.dma_start(
                 out=gain_bf[:], in_=ln1_gain.rearrange("(g p t) -> p g t", p=P, t=PACK)
@@ -74,53 +81,28 @@ def tile_swidtblock_pa_kernel(
             nc.scalar.dma_start(
                 out=lnb_bf[:], in_=ln1_bias.rearrange("(g p t) -> p g t", p=P, t=PACK)
             )
-        norm_cols = keep.tile([P, 2 * CHUNKS], F32)
-        nc.vector.tensor_copy(
-            out=norm_cols[:, 0:CHUNKS], in_=gain_bf[:].rearrange("p g t -> p (g t)")
-        )
-        nc.vector.tensor_copy(
-            out=norm_cols[:, CHUNKS : 2 * CHUNKS], in_=lnb_bf[:].rearrange("p g t -> p (g t)")
-        )
-        bias_rows = keep.tile([P, N_BLOCK], BF16)
-        nc.vector.memset(bias_rows[:], 0.0)
-        for w in range(3):
-            nc.scalar.dma_start(
-                out=bias_rows[BLOCKS_PER_WEIGHT * w : BLOCKS_PER_WEIGHT * (w + 1), :],
-                in_=biases[w].rearrange("(r c) -> r c", c=N_BLOCK),
-            )
-
-        x_sb = keep.tile([P, TOKEN_TILES, D], BF16)
-        w_raw = keep.tile([P, 3, PASSES, PACK, WIDTH], BF16)
-
-        def load_x(i):
-            nc.sync.dma_start(out=x_sb[:, i, :], in_=x_rows[P * i : P * (i + 1), :])
-
-        def load_w(w, g):
-            view = weights[w].rearrange("(g p t) n -> g p t n", t=PACK, p=P)
-            nc.sync.dma_start(out=w_raw[:, w, g, :, :], in_=view[g])
-
-        for i in range(HALF_TILES):
-            load_x(i)
+        load_x(1, 1)
+        load_x(2, 1)
+        load_x(3, 1)
         load_w(0, 0)
-        for i in range(HALF_TILES, TOKEN_TILES):
-            load_x(i)
+        load_x(4, 2)
+        load_x(6, 2)
         load_w(0, 1)
-        for w in range(1, 3):
-            for g in range(PASSES):
-                load_w(w, g)
+        load_w(1, 0)
+        load_w(1, 1)
+        for w in range(WEIGHTS):
+            nc.sync.dma_start(out=bias_all[:, w, :], in_=biases[w].partition_broadcast(P))
+        load_w(2, 0)
+        load_w(2, 1)
 
-        bias_all = keep.tile([P, BLOCKS * N_BLOCK], F32)
-        for b in range(BLOCKS):
-            bias_ps = psum.tile([P, N_BLOCK], F32, tag="acc")
-            nc.tensor.matmul(
-                out=bias_ps[:],
-                lhsT=ident_bf[:, b : b + 1].to_broadcast([P, P]),
-                rhs=bias_rows[:],
-                start=True,
-                stop=True,
-            )
-            nc.scalar.copy(out=bias_all[:, N_BLOCK * b : N_BLOCK * (b + 1)], in_=bias_ps[:])
+        eps_t = keep.tile([P, 1], F32)
+        nc.vector.memset(eps_t[:], EPS)
+        warm = keep.tile([P, 1], F32)
+        nc.scalar.activation(out=warm[:], in_=eps_t[:], func=ACT.Sqrt)
+        ident_f32 = keep.tile([P, P], F32)
+        make_identity(nc, ident_f32[:])
 
+        norm_cols = keep.tile([P, 2 * CHUNKS], F32)
         stats = keep.tile([P, TOKEN_TILES, D // STAT_PIECE, 6], F32)
         mean_var = keep.tile([P, TOKEN_TILES, 2], F32)
         std = keep.tile([P, TOKEN_TILES], F32)
@@ -128,7 +110,10 @@ def tile_swidtblock_pa_kernel(
         shift = keep.tile([P, TOKEN_TILES], F32)
         normed = keep.tile([P, TOKEN_TILES, D], F32)
 
-        def normalise(i):
+        neg_mean = keep.tile([P, 1], F32)
+        spread = keep.tile([P, 1], F32)
+
+        def statistics(i):
             for c in range(D // STAT_PIECE):
                 nc.vector.bn_stats(
                     out=stats[:, i, c, :], in_=x_sb[:, i, STAT_PIECE * c : STAT_PIECE * (c + 1)]
@@ -136,83 +121,134 @@ def tile_swidtblock_pa_kernel(
             nc.vector.bn_aggr(
                 out=mean_var[:, i, :], in_=stats[:, i, :, :].rearrange("p c s -> p (c s)")
             )
+
+        def deviation(i):
             nc.scalar.activation(
                 out=std[:, i : i + 1], in_=mean_var[:, i, 1:2], func=ACT.Sqrt, bias=eps_t[:, 0:1]
             )
-            nc.vector.reciprocal(out=rstd[:, i : i + 1], in_=std[:, i : i + 1])
+
+        def scalar_mean(i):
+            nc.scalar.activation(
+                out=normed[:, i, :],
+                in_=x_sb[:, i, :],
+                func=ACT.Identity,
+                scale=-1.0 / D,
+                accum_out=neg_mean[:, 0:1],
+            )
+
+        def scalar_deviation(i):
+            nc.scalar.activation(
+                out=normed[:, i, :],
+                in_=x_sb[:, i, :],
+                func=ACT.Square,
+                bias=neg_mean[:, 0:1],
+                accum_out=spread[:, 0:1],
+            )
+            nc.scalar.activation(
+                out=std[:, i : i + 1],
+                in_=spread[:, 0:1],
+                func=ACT.Sqrt,
+                scale=1.0 / D,
+                bias=eps_t[:, 0:1],
+            )
+
+        def scales(i):
+            one = slice(i, i + 1)
+            nc.vector.reciprocal(out=rstd[:, one], in_=std[:, one])
+            mean, sign = (neg_mean[:, 0:1], 1.0) if i == SCALAR_TILE else (mean_var[:, i, 0:1], -1.0)
             nc.vector.tensor_scalar(
-                out=shift[:, i : i + 1],
-                in0=mean_var[:, i, 0:1],
-                scalar1=rstd[:, i : i + 1],
-                scalar2=-1.0,
+                out=shift[:, one],
+                in0=mean,
+                scalar1=rstd[:, one],
+                scalar2=sign,
                 op0=ALU.mult,
                 op1=ALU.mult,
             )
-            nc.gpsimd.tensor_scalar(
-                out=normed[:, i, :].rearrange("p (g t q) -> p g t q", t=PACK, q=P),
-                in0=x_sb[:, i, :].rearrange("p (g q t) -> p g t q", t=PACK, q=P),
-                scalar1=rstd[:, i : i + 1],
-                scalar2=shift[:, i : i + 1],
-                op0=ALU.mult,
-                op1=ALU.add,
-            )
+
+        def normalise(i, on_scalar=False):
+            target = normed[:, i, :].rearrange("p (g t q) -> p g t q", t=PACK, q=P)
+            source = x_sb[:, i, :].rearrange("p (g q t) -> p g t q", t=PACK, q=P)
+            if on_scalar:
+                nc.scalar.activation(
+                    out=target,
+                    in_=source,
+                    func=ACT.Identity,
+                    bias=shift[:, i : i + 1],
+                    scale=rstd[:, i : i + 1],
+                )
+            else:
+                nc.gpsimd.tensor_scalar(
+                    out=target,
+                    in0=source,
+                    scalar1=rstd[:, i : i + 1],
+                    scalar2=shift[:, i : i + 1],
+                    op0=ALU.mult,
+                    op1=ALU.add,
+                )
 
         h_rows = keep.tile([P, 2, CHUNKS, HALF_TOKENS], BF16)
         h_codes = keep.tile([P, PASSES, TOKENS], U32, align_bytes=64)
         h_scales = keep.tile([P, PASSES, TOKENS], U8, align_bytes=64)
 
-        def transpose_and_scale(half):
-            for j in range(CHUNKS):
-                turned = psum.tile([P, HALF_TOKENS], F32, tag="turned")
-                for s in range(HALF_TILES):
-                    nc.tensor.transpose(
-                        turned[:, P * s : P * (s + 1)],
-                        normed[:, HALF_TILES * half + s, P * j : P * (j + 1)],
-                        ident_f32[:],
-                    )
-                nc.scalar.activation(
-                    out=h_rows[:, half, j, :],
-                    in_=turned[:],
-                    func=ACT.Identity,
-                    bias=norm_cols[:, CHUNKS + j : CHUNKS + j + 1],
-                    scale=norm_cols[:, j : j + 1],
+        def transpose(half, j):
+            turned = psum.tile([P, HALF_TOKENS], F32, tag="bank")
+            for s in range(HALF_TILES):
+                nc.tensor.transpose(
+                    turned[:, P * s : P * (s + 1)],
+                    normed[:, HALF_TILES * half + s, P * j : P * (j + 1)],
+                    ident_f32[:],
                 )
+            return turned
 
-        def quantise_h(half):
-            tokens = slice(HALF_TOKENS * half, HALF_TOKENS * (half + 1))
-            for g in range(PASSES):
-                grouped_h = h_stage.tile([P, HALF_TOKENS, PACK], BF16, align_bytes=64)
-                regroup(nc.vector.tensor_copy, grouped_h[:], h_rows[:, half, PACK * g : PACK * (g + 1), :])
-                nc.vector.quantize_mx(
-                    out=h_codes[:, g, tokens].bitcast(FP8X4),
-                    scales=h_scales[:, g, tokens],
-                    in_=grouped_h[:].rearrange("p r t -> p (r t)"),
-                )
-
-        w_codes = keep.tile([P, PASSES, BLOCKS * N_BLOCK], U32, align_bytes=64)
-        w_scales = keep.tile([P, PASSES, BLOCKS * N_BLOCK], U8, align_bytes=64)
-
-        def regroup_w(b, g):
-            w, part = divmod(b, BLOCKS_PER_WEIGHT)
-            grouped_w = w_stage.tile([P, N_BLOCK, PACK], BF16, align_bytes=64)
-            regroup(
-                nc.scalar.copy, grouped_w[:], w_raw[:, w, g, :, N_BLOCK * part : N_BLOCK * (part + 1)]
+        def scale_and_shift(half, j, turned):
+            nc.scalar.activation(
+                out=h_rows[:, half, j, :],
+                in_=turned[:],
+                func=ACT.Identity,
+                bias=norm_cols[:, CHUNKS + j : CHUNKS + j + 1],
+                scale=norm_cols[:, j : j + 1],
             )
+
+        def regroup_h(half, g):
+            grouped_h = h_stage.tile([P, HALF_TOKENS, PACK], BF16, align_bytes=64)
+            regroup(
+                nc.vector.tensor_copy, grouped_h[:], h_rows[:, half, PACK * g : PACK * (g + 1), :]
+            )
+            return grouped_h
+
+        def quantise_h(half, g, grouped_h):
+            tokens = slice(HALF_TOKENS * half, HALF_TOKENS * (half + 1))
+            nc.vector.quantize_mx(
+                out=h_codes[:, g, tokens].bitcast(FP8X4),
+                scales=h_scales[:, g, tokens],
+                in_=grouped_h[:].rearrange("p r t -> p (r t)"),
+            )
+
+        w_codes = keep.tile([P, PASSES, WEIGHTS * WIDTH], U32, align_bytes=64)
+        w_scales = keep.tile([P, PASSES, WEIGHTS * WIDTH], U8, align_bytes=64)
+
+        def w_tile():
+            grouped_w = w_stage.tile([P, N_BLOCK, PACK], BF16, align_bytes=64)
             return grouped_w
 
-        def quantise_w(b, g, grouped_w):
-            cols = slice(N_BLOCK * b, N_BLOCK * (b + 1))
+        def regroup_w(copy, tile, w, g, part, first=0, width=N_BLOCK):
+            source = N_BLOCK * part + first
+            regroup(copy, tile[:, first : first + width, :], w_raw[:, w, g, :, source : source + width])
+
+        def quantise_w(w, g, part, grouped_w):
+            first = WIDTH * w + N_BLOCK * part
+            cols = slice(first, first + N_BLOCK)
             nc.vector.quantize_mx(
                 out=w_codes[:, g, cols].bitcast(FP8X4),
                 scales=w_scales[:, g, cols],
                 in_=grouped_w[:].rearrange("p c t -> p (c t)"),
             )
 
-        def project(b, i):
-            w, part = divmod(b, BLOCKS_PER_WEIGHT)
-            cols = slice(N_BLOCK * b, N_BLOCK * (b + 1))
+        def multiply(w, part, i):
+            first = WIDTH * w + N_BLOCK * part
+            cols = slice(first, first + N_BLOCK)
             tokens = slice(P * i, P * (i + 1))
-            acc = psum.tile([P, N_BLOCK], F32, tag="acc")
+            acc = psum.tile([P, N_BLOCK], F32, tag="bank")
             for g in range(PASSES):
                 nc.tensor.matmul_mx(
                     out=acc[:],
@@ -223,37 +259,141 @@ def tile_swidtblock_pa_kernel(
                     start=(g == 0),
                     stop=(g == PASSES - 1),
                 )
-            result = o_stage.tile([P, N_BLOCK], F32)
-            if i % SCALAR_SHARE == SCALAR_SHARE - 1:
-                nc.scalar.copy(out=result[:], in_=acc[:])
-                nc.gpsimd.tensor_tensor(
-                    out=result[:], in0=result[:], in1=bias_all[:, cols], op=ALU.add
-                )
-            else:
-                nc.vector.tensor_tensor(
-                    out=result[:], in0=acc[:], in1=bias_all[:, cols], op=ALU.add
-                )
-            nc.sync.dma_start(
-                out=outs[w][tokens, N_BLOCK * part : N_BLOCK * (part + 1)], in_=result[:]
+            return acc
+
+        def add_bias(w, part, acc, result):
+            cols = slice(N_BLOCK * part, N_BLOCK * (part + 1))
+            nc.vector.tensor_tensor(
+                out=result[:, cols], in0=acc[:], in1=bias_all[:, w, cols], op=ALU.add
             )
 
-        for i in range(HALF_TILES):
-            normalise(i)
-        first_0 = regroup_w(0, 0)
-        for i in range(HALF_TILES, TOKEN_TILES):
-            normalise(i)
-        transpose_and_scale(0)
-        first_1 = regroup_w(0, 1)
-        quantise_h(0)
-        quantise_w(0, 0, first_0)
-        quantise_w(0, 1, first_1)
-        transpose_and_scale(1)
-        quantise_h(1)
-        for b in range(BLOCKS):
-            for g in range(PASSES):
-                if b + 1 < BLOCKS:
-                    grouped_next = regroup_w(b + 1, g)
-                for i in range(HALF_TILES * g, HALF_TILES * (g + 1)):
-                    project(b, i)
-                if b + 1 < BLOCKS:
-                    quantise_w(b + 1, g, grouped_next)
+        def store(w, i, result, first=0, width=WIDTH):
+            nc.sync.dma_start(
+                out=outs[w][P * i : P * (i + 1), first : first + width],
+                in_=result[:, first : first + width],
+            )
+
+        def project(w, part, i, on_scalar=False):
+            acc = multiply(w, part, i)
+            result = o_stage.tile([P, N_BLOCK], F32, tag="result")
+            bias = bias_all[:, w, N_BLOCK * part : N_BLOCK * (part + 1)]
+            if on_scalar:
+                nc.scalar.copy(out=result[:], in_=acc[:])
+                nc.gpsimd.tensor_tensor(out=result[:], in0=result[:], in1=bias, op=ALU.add)
+            else:
+                nc.vector.tensor_tensor(out=result[:], in0=acc[:], in1=bias, op=ALU.add)
+            return w, part, i, result
+
+        def store(w, part, i, result):
+            nc.sync.dma_start(
+                out=outs[w][P * i : P * (i + 1), N_BLOCK * part : N_BLOCK * (part + 1)],
+                in_=result[:],
+            )
+
+        v_copy = nc.vector.tensor_copy
+        s_copy = nc.scalar.copy
+        quarter = N_BLOCK // 2
+
+        w00 = w_tile()
+        w01 = w_tile()
+        statistics(0)
+        scalar_mean(1)
+        deviation(0)
+        scalar_deviation(1)
+        statistics(2)
+        deviation(2)
+        scales(0)
+        normalise(0)
+        statistics(3)
+        deviation(3)
+        scales(2)
+        normalise(2)
+        scales(1)
+        normalise(1, True)
+        statistics(4)
+        scales(3)
+        normalise(3)
+        regroup_w(s_copy, w00, 0, 0, 0, 0, quarter)
+        deviation(4)
+        statistics(5)
+        scales(4)
+        normalise(4)
+        regroup_w(s_copy, w00, 0, 0, 0, quarter, quarter)
+        deviation(5)
+        statistics(6)
+        scales(5)
+        normalise(5)
+        nc.vector.tensor_copy(
+            out=norm_cols[:, 0:CHUNKS], in_=gain_bf[:].rearrange("p g t -> p (g t)")
+        )
+        nc.vector.tensor_copy(
+            out=norm_cols[:, CHUNKS : 2 * CHUNKS], in_=lnb_bf[:].rearrange("p g t -> p (g t)")
+        )
+        for j in range(2):
+            scale_and_shift(0, j, transpose(0, j))
+        deviation(6)
+        statistics(7)
+        scales(6)
+        normalise(6)
+        for j in range(2, 4):
+            scale_and_shift(0, j, transpose(0, j))
+        deviation(7)
+        for j in range(4, 8):
+            scale_and_shift(0, j, transpose(0, j))
+        h00 = regroup_h(0, 0)
+        scales(7)
+        normalise(7)
+        regroup_w(v_copy, w01, 0, 1, 0)
+        quantise_h(0, 0, h00)
+        quantise_w(0, 0, 0, w00)
+        h01 = regroup_h(0, 1)
+        quantise_w(0, 1, 0, w01)
+        quantise_h(0, 1, h01)
+        for j in range(CHUNKS):
+            scale_and_shift(1, j, transpose(1, j))
+        h10 = regroup_h(1, 0)
+        grouped = {}
+
+        def prepare(w, part, g):
+            tile = w_tile()
+            regroup_w(s_copy, tile, w, g, part)
+            grouped[w, part, g] = tile
+
+        def quantise_next(w, part, g):
+            quantise_w(w, g, part, grouped[w, part, g])
+
+        order = [(w, part) for w in range(WEIGHTS) for part in range(PARTS)]
+        pieces = [(w, part, g) for w, part in order[1:] for g in range(PASSES)]
+        prepare(*pieces[0])
+        prepare(*pieces[1])
+        for i in range(4):
+            store(*project(0, 0, i))
+        h11 = regroup_h(1, 1)
+        quantise_h(1, 0, h10)
+        quantise_h(1, 1, h11)
+        prepare(*pieces[2])
+        for i in range(4, 8):
+            store(*project(0, 0, i))
+            if i in (4, 5):
+                quantise_next(*pieces[i - 4])
+        prepared, quantised = 3, 2
+        on_scalar = {1: (3, 6), 2: (1, 4, 6), 3: (1, 4, 6), 4: (1, 4), 5: (0, 2, 4)}
+        held = []
+        for n in range(1, len(order)):
+            for i in range(TOKEN_TILES):
+                if i in (0, 5) and prepared < len(pieces):
+                    prepare(*pieces[prepared])
+                    prepared += 1
+                result = project(*order[n], i, on_scalar=i in on_scalar[n])
+                if i in on_scalar[n]:
+                    held.append(result)
+                else:
+                    store(*result)
+                    if held and (len(held) > 1 or i - 3 >= held[0][2]):
+                        store(*held.pop(0))
+                if i in (1, 4) and quantised < len(pieces):
+                    quantise_next(*pieces[quantised])
+                    quantised += 1
+            if n + 1 == len(order):
+                while held:
+                    store(*held.pop(0))

@@ -28,7 +28,6 @@ PARTS = WIDTH // N_BLOCK
 STAT_PIECE = 512
 RUN = 4
 EPS = 1e-6
-SCALAR_TILE = 1
 
 FLOPS = 2 * TOKENS * D * WEIGHTS * WIDTH
 
@@ -53,7 +52,7 @@ def tile_swidtblock_pa_kernel(
         keep = ctx.enter_context(tc.tile_pool(name="keep", bufs=1))
         h_stage = ctx.enter_context(tc.tile_pool(name="h_stage", bufs=2))
         w_stage = ctx.enter_context(tc.tile_pool(name="w_stage", bufs=4))
-        o_stage = ctx.enter_context(tc.tile_pool(name="o_stage", bufs=12))
+        o_stage = ctx.enter_context(tc.tile_pool(name="o_stage", bufs=16))
         psum = ctx.enter_context(tc.psum_pool(name="psum", bufs=8))
         ctx.enter_context(tc.manual_schedule())
 
@@ -89,102 +88,62 @@ def tile_swidtblock_pa_kernel(
         load_x(6, 2)
         load_w(0, 1)
         load_w(1, 0)
-        load_w(1, 1)
         for w in range(WEIGHTS):
             nc.sync.dma_start(out=bias_all[:, w, :], in_=biases[w].partition_broadcast(P))
+        load_w(1, 1)
         load_w(2, 0)
         load_w(2, 1)
 
         eps_t = keep.tile([P, 1], F32)
         nc.vector.memset(eps_t[:], EPS)
         warm = keep.tile([P, 1], F32)
-        nc.scalar.activation(out=warm[:], in_=eps_t[:], func=ACT.Sqrt)
+        nc.scalar.activation(out=warm[:], in_=eps_t[:], func=ACT.Abs_reciprocal_sqrt)
         ident_f32 = keep.tile([P, P], F32)
         make_identity(nc, ident_f32[:])
 
         norm_cols = keep.tile([P, 2 * CHUNKS], F32)
         stats = keep.tile([P, TOKEN_TILES, D // STAT_PIECE, 6], F32)
         mean_var = keep.tile([P, TOKEN_TILES, 2], F32)
-        std = keep.tile([P, TOKEN_TILES], F32)
         rstd = keep.tile([P, TOKEN_TILES], F32)
-        shift = keep.tile([P, TOKEN_TILES], F32)
+        shift_g = keep.tile([P, TOKEN_TILES], F32)
+        shift_v = keep.tile([P, TOKEN_TILES], F32)
         normed = keep.tile([P, TOKEN_TILES, D], F32)
 
-        neg_mean = keep.tile([P, 1], F32)
-        spread = keep.tile([P, 1], F32)
+        def statistics(i, c):
+            nc.vector.bn_stats(
+                out=stats[:, i, c, :], in_=x_sb[:, i, STAT_PIECE * c : STAT_PIECE * (c + 1)]
+            )
 
-        def statistics(i):
-            for c in range(D // STAT_PIECE):
-                nc.vector.bn_stats(
-                    out=stats[:, i, c, :], in_=x_sb[:, i, STAT_PIECE * c : STAT_PIECE * (c + 1)]
-                )
+        def aggregate(i):
             nc.vector.bn_aggr(
                 out=mean_var[:, i, :], in_=stats[:, i, :, :].rearrange("p c s -> p (c s)")
             )
 
         def deviation(i):
             nc.scalar.activation(
-                out=std[:, i : i + 1], in_=mean_var[:, i, 1:2], func=ACT.Sqrt, bias=eps_t[:, 0:1]
-            )
-
-        def scalar_mean(i):
-            nc.scalar.activation(
-                out=normed[:, i, :],
-                in_=x_sb[:, i, :],
-                func=ACT.Identity,
-                scale=-1.0 / D,
-                accum_out=neg_mean[:, 0:1],
-            )
-
-        def scalar_deviation(i):
-            nc.scalar.activation(
-                out=normed[:, i, :],
-                in_=x_sb[:, i, :],
-                func=ACT.Square,
-                bias=neg_mean[:, 0:1],
-                accum_out=spread[:, 0:1],
-            )
-            nc.scalar.activation(
-                out=std[:, i : i + 1],
-                in_=spread[:, 0:1],
-                func=ACT.Sqrt,
-                scale=1.0 / D,
+                out=rstd[:, i : i + 1],
+                in_=mean_var[:, i, 1:2],
+                func=ACT.Abs_reciprocal_sqrt,
                 bias=eps_t[:, 0:1],
             )
 
-        def scales(i):
-            one = slice(i, i + 1)
-            nc.vector.reciprocal(out=rstd[:, one], in_=std[:, one])
-            mean, sign = (neg_mean[:, 0:1], 1.0) if i == SCALAR_TILE else (mean_var[:, i, 0:1], -1.0)
-            nc.vector.tensor_scalar(
-                out=shift[:, one],
-                in0=mean,
-                scalar1=rstd[:, one],
-                scalar2=sign,
+        def normalise(engine, shift, i):
+            engine.tensor_scalar(
+                out=shift[:, i : i + 1],
+                in0=mean_var[:, i, 0:1],
+                scalar1=rstd[:, i : i + 1],
+                scalar2=-1.0,
                 op0=ALU.mult,
                 op1=ALU.mult,
             )
-
-        def normalise(i, on_scalar=False):
-            target = normed[:, i, :].rearrange("p (g t q) -> p g t q", t=PACK, q=P)
-            source = x_sb[:, i, :].rearrange("p (g q t) -> p g t q", t=PACK, q=P)
-            if on_scalar:
-                nc.scalar.activation(
-                    out=target,
-                    in_=source,
-                    func=ACT.Identity,
-                    bias=shift[:, i : i + 1],
-                    scale=rstd[:, i : i + 1],
-                )
-            else:
-                nc.gpsimd.tensor_scalar(
-                    out=target,
-                    in0=source,
-                    scalar1=rstd[:, i : i + 1],
-                    scalar2=shift[:, i : i + 1],
-                    op0=ALU.mult,
-                    op1=ALU.add,
-                )
+            engine.tensor_scalar(
+                out=normed[:, i, :].rearrange("p (g t q) -> p g t q", t=PACK, q=P),
+                in0=x_sb[:, i, :].rearrange("p (g q t) -> p g t q", t=PACK, q=P),
+                scalar1=rstd[:, i : i + 1],
+                scalar2=shift[:, i : i + 1],
+                op0=ALU.mult,
+                op1=ALU.add,
+            )
 
         h_rows = keep.tile([P, 2, CHUNKS, HALF_TOKENS], BF16)
         h_codes = keep.tile([P, PASSES, TOKENS], U32, align_bytes=64)
@@ -294,95 +253,78 @@ def tile_swidtblock_pa_kernel(
         s_copy = nc.scalar.copy
         quarter = N_BLOCK // 2
 
-        w00 = w_tile()
-        w01 = w_tile()
-        statistics(0)
-        scalar_mean(1)
-        deviation(0)
-        scalar_deviation(1)
-        statistics(2)
-        deviation(2)
-        scales(0)
-        normalise(0)
-        statistics(3)
-        deviation(3)
-        scales(2)
-        normalise(2)
-        scales(1)
-        normalise(1, True)
-        statistics(4)
-        scales(3)
-        normalise(3)
-        regroup_w(s_copy, w00, 0, 0, 0, 0, quarter)
-        deviation(4)
-        statistics(5)
-        scales(4)
-        normalise(4)
-        regroup_w(s_copy, w00, 0, 0, 0, quarter, quarter)
-        deviation(5)
-        statistics(6)
-        scales(5)
-        normalise(5)
+        grouped = {}
+
+        def prepare(copy, w, part, g, first=0, width=N_BLOCK):
+            if first == 0:
+                grouped[w, part, g] = w_tile()
+            regroup_w(copy, grouped[w, part, g], w, g, part, first, width)
+
+        def quantise_piece(w, part, g):
+            quantise_w(w, g, part, grouped[w, part, g])
+
+        statistics(0, 0)
+        statistics(0, 1)
+        for i in range(1, TOKEN_TILES):
+            statistics(i, 0)
+            aggregate(i - 1)
+            deviation(i - 1)
+            if i < 7:
+                normalise(nc.gpsimd, shift_g, i - 1)
+            statistics(i, 1)
+            if i == 3:
+                prepare(s_copy, 0, 0, 0, 0, quarter)
+            if i == 4:
+                prepare(s_copy, 0, 0, 0, quarter, quarter)
+            if i == 5:
+                prepare(s_copy, 0, 1, 0, 0, quarter)
+            if i == 6:
+                prepare(s_copy, 0, 1, 0, quarter, quarter)
         nc.vector.tensor_copy(
             out=norm_cols[:, 0:CHUNKS], in_=gain_bf[:].rearrange("p g t -> p (g t)")
         )
+        aggregate(7)
         nc.vector.tensor_copy(
             out=norm_cols[:, CHUNKS : 2 * CHUNKS], in_=lnb_bf[:].rearrange("p g t -> p (g t)")
         )
-        for j in range(2):
+        for j in range(CHUNKS):
             scale_and_shift(0, j, transpose(0, j))
-        deviation(6)
-        statistics(7)
-        scales(6)
-        normalise(6)
-        for j in range(2, 4):
-            scale_and_shift(0, j, transpose(0, j))
-        deviation(7)
-        for j in range(4, 8):
-            scale_and_shift(0, j, transpose(0, j))
+            if j == 0:
+                deviation(7)
+        normalise(nc.vector, shift_v, 6)
+        normalise(nc.vector, shift_v, 7)
+        prepare(v_copy, 0, 0, 1)
         h00 = regroup_h(0, 0)
-        scales(7)
-        normalise(7)
-        regroup_w(v_copy, w01, 0, 1, 0)
+        quantise_piece(0, 0, 0)
         quantise_h(0, 0, h00)
-        quantise_w(0, 0, 0, w00)
         h01 = regroup_h(0, 1)
-        quantise_w(0, 1, 0, w01)
+        quantise_piece(0, 0, 1)
         quantise_h(0, 1, h01)
         for j in range(CHUNKS):
             scale_and_shift(1, j, transpose(1, j))
+        prepare(s_copy, 0, 1, 1)
+        prepare(s_copy, 1, 0, 0)
+        prepare(s_copy, 1, 0, 1)
         h10 = regroup_h(1, 0)
-        grouped = {}
-
-        def prepare(w, part, g):
-            tile = w_tile()
-            regroup_w(s_copy, tile, w, g, part)
-            grouped[w, part, g] = tile
-
-        def quantise_next(w, part, g):
-            quantise_w(w, g, part, grouped[w, part, g])
-
-        order = [(w, part) for w in range(WEIGHTS) for part in range(PARTS)]
-        pieces = [(w, part, g) for w, part in order[1:] for g in range(PASSES)]
-        prepare(*pieces[0])
-        prepare(*pieces[1])
         for i in range(4):
             store(*project(0, 0, i))
         h11 = regroup_h(1, 1)
         quantise_h(1, 0, h10)
+        quantise_piece(0, 1, 0)
         quantise_h(1, 1, h11)
-        prepare(*pieces[2])
         for i in range(4, 8):
             store(*project(0, 0, i))
-            if i in (4, 5):
-                quantise_next(*pieces[i - 4])
-        prepared, quantised = 3, 2
-        on_scalar = {1: (3, 6), 2: (1, 4, 6), 3: (1, 4, 6), 4: (1, 4), 5: (0, 2, 4)}
+            if i == 5:
+                quantise_piece(0, 1, 1)
+        order = [(w, part) for w in range(WEIGHTS) for part in range(PARTS)]
+        pieces = [(w, part, g) for w, part in order[1:] for g in range(PASSES)]
+        prepared, quantised = 4, 2
+        on_scalar = {1: (2, 5), 2: (2, 5), 3: (2, 5), 4: (1, 4), 5: (0, 2, 4)}
         held = []
         for n in range(1, len(order)):
             for i in range(TOKEN_TILES):
-                if i in (0, 5) and prepared < len(pieces):
-                    prepare(*pieces[prepared])
+                if i in (0, 4) and prepared < len(pieces):
+                    prepare(s_copy, *pieces[prepared])
                     prepared += 1
                 result = project(*order[n], i, on_scalar=i in on_scalar[n])
                 if i in on_scalar[n]:
@@ -391,9 +333,8 @@ def tile_swidtblock_pa_kernel(
                     store(*result)
                     if held and (len(held) > 1 or i - 3 >= held[0][2]):
                         store(*held.pop(0))
-                if i in (1, 4) and quantised < len(pieces):
-                    quantise_next(*pieces[quantised])
+                if i in (0, 3) and quantised < len(pieces):
+                    quantise_piece(*pieces[quantised])
                     quantised += 1
-            if n + 1 == len(order):
-                while held:
-                    store(*held.pop(0))
+        for result in held:
+            store(*result)

@@ -302,13 +302,14 @@ def tile_swidtblock_pa_kernel(
         quantise_h(0, 1, h01)
         for j in range(CHUNKS):
             scale_and_shift(1, j, transpose(1, j))
+        h11 = h_stage.tile([P, HALF_TOKENS, PACK], BF16, align_bytes=64)
+        regroup(s_copy, h11[:], h_rows[:, 1, PACK : 2 * PACK, :])
         prepare(s_copy, 0, 1, 1)
         prepare(s_copy, 1, 0, 0)
         prepare(s_copy, 1, 0, 1)
         h10 = regroup_h(1, 0)
         for i in range(4):
             store(*project(0, 0, i))
-        h11 = regroup_h(1, 1)
         quantise_h(1, 0, h10)
         quantise_piece(0, 1, 0)
         quantise_h(1, 1, h11)
@@ -319,22 +320,12 @@ def tile_swidtblock_pa_kernel(
         order = [(w, part) for w in range(WEIGHTS) for part in range(PARTS)]
         pieces = [(w, part, g) for w, part in order[1:] for g in range(PASSES)]
         prepared, quantised = 4, 2
-        on_scalar = {1: (2, 5), 2: (2, 5), 3: (2, 5), 4: (1, 4), 5: (0, 2, 4)}
-        held = []
         for n in range(1, len(order)):
             for i in range(TOKEN_TILES):
                 if i in (0, 4) and prepared < len(pieces):
                     prepare(s_copy, *pieces[prepared])
                     prepared += 1
-                result = project(*order[n], i, on_scalar=i in on_scalar[n])
-                if i in on_scalar[n]:
-                    held.append(result)
-                else:
-                    store(*result)
-                    if held and (len(held) > 1 or i - 3 >= held[0][2]):
-                        store(*held.pop(0))
+                store(*project(*order[n], i))
                 if i in (0, 3) and quantised < len(pieces):
                     quantise_piece(*pieces[quantised])
                     quantised += 1
-        for result in held:
-            store(*result)

from contextlib import ExitStack

import concourse.mybir as mybir
from concourse.masks import make_identity

F32 = mybir.dt.float32
BF16 = mybir.dt.bfloat16
U32 = mybir.dt.uint32
U8 = mybir.dt.uint8
FP8X4 = mybir.dt.float8_e4m3fn_x4
ALU = mybir.AluOpType
ACT = mybir.ActivationFunctionType

P = 128
PACK = 4
K_PASS = P * PACK
D = 1024
PASSES = D // K_PASS
CHUNKS = D // P
TOKENS = 1024
TOKEN_TILES = TOKENS // P
HALF_TILES = TOKEN_TILES // 2
HALF_TOKENS = HALF_TILES * P
WIDTH = 1024
WEIGHTS = 3
N_BLOCK = 512
PARTS = WIDTH // N_BLOCK
STAT_PIECE = 512
RUN = 4
EPS = 1e-6

FLOPS = 2 * TOKENS * D * WEIGHTS * WIDTH


def regroup(copy, grouped, rows):
    copy(
        out=grouped.rearrange("p (c i) t -> p c t i", i=RUN),
        in_=rows.rearrange("p t (c i) -> p c t i", i=RUN),
    )


def tile_swidtblock_pa_kernel(
    tc, x, ln1_gain, ln1_bias, wq, bq, wk, bk, wv, bv, out_0, out_1, out_2
):
    nc = tc.nc
    x_rows = x.flatten_outer_dims()
    weights = [wq, wk, wv]
    biases = [bq, bk, bv]
    outs = [o.rearrange("b t h e -> (b t) (h e)") for o in (out_0, out_1, out_2)]

    with ExitStack() as ctx:
        keep = ctx.enter_context(tc.tile_pool(name="keep", bufs=1))
        h_stage = ctx.enter_context(tc.tile_pool(name="h_stage", bufs=2))
        w_stage = ctx.enter_context(tc.tile_pool(name="w_stage", bufs=4))
        o_stage = ctx.enter_context(tc.tile_pool(name="o_stage", bufs=16))
        psum = ctx.enter_context(tc.psum_pool(name="psum", bufs=8))
        ctx.enter_context(tc.manual_schedule())

        x_sb = keep.tile([P, TOKEN_TILES, D], BF16)
        w_raw = keep.tile([P, WEIGHTS, PASSES, PACK, WIDTH], BF16)
        gain_bf = keep.tile([P, PASSES, PACK], BF16)
        lnb_bf = keep.tile([P, PASSES, PACK], BF16)
        bias_all = keep.tile([P, WEIGHTS, WIDTH], BF16)

        def load_x(first, count):
            nc.sync.dma_start(
                out=x_sb[:, first : first + count, :],
                in_=x_rows[P * first : P * (first + count), :].rearrange("(i p) d -> p i d", p=P),
            )

        def load_w(w, g):
            view = weights[w].rearrange("(g p t) n -> g p t n", t=PACK, p=P)
            nc.sync.dma_start(out=w_raw[:, w, g, :, :], in_=view[g])

        load_x(0, 1)
        with nc.allow_non_contiguous_dma(reason="four neighbouring values a partition"):
            nc.scalar.dma_start(
                out=gain_bf[:], in_=ln1_gain.rearrange("(g p t) -> p g t", p=P, t=PACK)
            )
            nc.scalar.dma_start(
                out=lnb_bf[:], in_=ln1_bias.rearrange("(g p t) -> p g t", p=P, t=PACK)
            )
        load_x(1, 1)
        load_x(2, 1)
        load_x(3, 1)
        load_w(0, 0)
        load_x(4, 2)
        load_x(6, 2)
        load_w(0, 1)
        load_w(1, 0)
        for w in range(WEIGHTS):
            nc.sync.dma_start(out=bias_all[:, w, :], in_=biases[w].partition_broadcast(P))
        load_w(1, 1)
        load_w(2, 0)
        load_w(2, 1)

        eps_t = keep.tile([P, 1], F32)
        nc.vector.memset(eps_t[:], EPS)
        warm = keep.tile([P, 1], F32)
        nc.scalar.activation(out=warm[:], in_=eps_t[:], func=ACT.Abs_reciprocal_sqrt)
        ident_f32 = keep.tile([P, P], F32)
        make_identity(nc, ident_f32[:])

        norm_cols = keep.tile([P, 2 * CHUNKS], F32)
        stats = keep.tile([P, TOKEN_TILES, D // STAT_PIECE, 6], F32)
        mean_var = keep.tile([P, TOKEN_TILES, 2], F32)
        rstd = keep.tile([P, TOKEN_TILES], F32)
        shift_g = keep.tile([P, TOKEN_TILES], F32)
        shift_v = keep.tile([P, TOKEN_TILES], F32)
        normed = keep.tile([P, TOKEN_TILES, D], F32)

        def statistics(i, c):
            nc.vector.bn_stats(
                out=stats[:, i, c, :], in_=x_sb[:, i, STAT_PIECE * c : STAT_PIECE * (c + 1)]
            )

        def aggregate(i):
            nc.vector.bn_aggr(
                out=mean_var[:, i, :], in_=stats[:, i, :, :].rearrange("p c s -> p (c s)")
            )

        def deviation(i):
            nc.scalar.activation(
                out=rstd[:, i : i + 1],
                in_=mean_var[:, i, 1:2],
                func=ACT.Abs_reciprocal_sqrt,
                bias=eps_t[:, 0:1],
            )

        def normalise(engine, shift, i):
            engine.tensor_scalar(
                out=shift[:, i : i + 1],
                in0=mean_var[:, i, 0:1],
                scalar1=rstd[:, i : i + 1],
                scalar2=-1.0,
                op0=ALU.mult,
                op1=ALU.mult,
            )
            engine.tensor_scalar(
                out=normed[:, i, :].rearrange("p (g t q) -> p g t q", t=PACK, q=P),
                in0=x_sb[:, i, :].rearrange("p (g q t) -> p g t q", t=PACK, q=P),
                scalar1=rstd[:, i : i + 1],
                scalar2=shift[:, i : i + 1],
                op0=ALU.mult,
                op1=ALU.add,
            )

        h_rows = keep.tile([P, 2, CHUNKS, HALF_TOKENS], BF16)
        h_codes = keep.tile([P, PASSES, TOKENS], U32, align_bytes=64)
        h_scales = keep.tile([P, PASSES, TOKENS], U8, align_bytes=64)

        def transpose(half, j):
            turned = psum.tile([P, HALF_TOKENS], F32, tag="bank")
            for s in range(HALF_TILES):
                nc.tensor.transpose(
                    turned[:, P * s : P * (s + 1)],
                    normed[:, HALF_TILES * half + s, P * j : P * (j + 1)],
                    ident_f32[:],
                )
            return turned

        def scale_and_shift(half, j, turned):
            nc.scalar.activation(
                out=h_rows[:, half, j, :],
                in_=turned[:],
                func=ACT.Identity,
                bias=norm_cols[:, CHUNKS + j : CHUNKS + j + 1],
                scale=norm_cols[:, j : j + 1],
            )

        def regroup_h(half, g):
            grouped_h = h_stage.tile([P, HALF_TOKENS, PACK], BF16, align_bytes=64)
            regroup(
                nc.vector.tensor_copy, grouped_h[:], h_rows[:, half, PACK * g : PACK * (g + 1), :]
            )
            return grouped_h

        def quantise_h(half, g, grouped_h):
            tokens = slice(HALF_TOKENS * half, HALF_TOKENS * (half + 1))
            nc.vector.quantize_mx(
                out=h_codes[:, g, tokens].bitcast(FP8X4),
                scales=h_scales[:, g, tokens],
                in_=grouped_h[:].rearrange("p r t -> p (r t)"),
            )

        w_codes = keep.tile([P, PASSES, WEIGHTS * WIDTH], U32, align_bytes=64)
        w_scales = keep.tile([P, PASSES, WEIGHTS * WIDTH], U8, align_bytes=64)

        def w_tile():
            grouped_w = w_stage.tile([P, N_BLOCK, PACK], BF16, align_bytes=64)
            return grouped_w

        def regroup_w(copy, tile, w, g, part, first=0, width=N_BLOCK):
            source = N_BLOCK * part + first
            regroup(copy, tile[:, first : first + width, :], w_raw[:, w, g, :, source : source + width])

        def quantise_w(w, g, part, grouped_w):
            first = WIDTH * w + N_BLOCK * part
            cols = slice(first, first + N_BLOCK)
            nc.vector.quantize_mx(
                out=w_codes[:, g, cols].bitcast(FP8X4),
                scales=w_scales[:, g, cols],
                in_=grouped_w[:].rearrange("p c t -> p (c t)"),
            )

        def multiply(w, part, i):
            first = WIDTH * w + N_BLOCK * part
            cols = slice(first, first + N_BLOCK)
            tokens = slice(P * i, P * (i + 1))
            acc = psum.tile([P, N_BLOCK], F32, tag="bank")
            for g in range(PASSES):
                nc.tensor.matmul_mx(
                    out=acc[:],
                    lhsT=h_codes[:, g, tokens].bitcast(FP8X4),
                    lhsT_scale=h_scales[:, g, tokens],
                    rhs=w_codes[:, g, cols].bitcast(FP8X4),
                    rhs_scale=w_scales[:, g, cols],
                    start=(g == 0),
                    stop=(g == PASSES - 1),
                )
            return acc

        def add_bias(w, part, acc, result):
            cols = slice(N_BLOCK * part, N_BLOCK * (part + 1))
            nc.vector.tensor_tensor(
                out=result[:, cols], in0=acc[:], in1=bias_all[:, w, cols], op=ALU.add
            )

        def store(w, i, result, first=0, width=WIDTH):
            nc.sync.dma_start(
                out=outs[w][P * i : P * (i + 1), first : first + width],
                in_=result[:, first : first + width],
            )

        def project(w, part, i, on_scalar=False):
            acc = multiply(w, part, i)
            result = o_stage.tile([P, N_BLOCK], F32, tag="result")
            bias = bias_all[:, w, N_BLOCK * part : N_BLOCK * (part + 1)]
            if on_scalar:
                nc.scalar.copy(out=result[:], in_=acc[:])
                nc.gpsimd.tensor_tensor(out=result[:], in0=result[:], in1=bias, op=ALU.add)
            else:
                nc.vector.tensor_tensor(out=result[:], in0=acc[:], in1=bias, op=ALU.add)
            return w, part, i, result

        def store(w, part, i, result):
            nc.sync.dma_start(
                out=outs[w][P * i : P * (i + 1), N_BLOCK * part : N_BLOCK * (part + 1)],
                in_=result[:],
            )

        v_copy = nc.vector.tensor_copy
        s_copy = nc.scalar.copy
        quarter = N_BLOCK // 2

        grouped = {}

        def prepare(copy, w, part, g, first=0, width=N_BLOCK):
            if first == 0:
                grouped[w, part, g] = w_tile()
            regroup_w(copy, grouped[w, part, g], w, g, part, first, width)

        def quantise_piece(w, part, g):
            quantise_w(w, g, part, grouped[w, part, g])

        statistics(0, 0)
        statistics(0, 1)
        for i in range(1, TOKEN_TILES):
            statistics(i, 0)
            aggregate(i - 1)
            deviation(i - 1)
            if i < 7:
                normalise(nc.gpsimd, shift_g, i - 1)
            statistics(i, 1)
            if i == 3:
                prepare(s_copy, 0, 0, 0, 0, quarter)
            if i == 4:
                prepare(s_copy, 0, 0, 0, quarter, quarter)
            if i == 5:
                prepare(s_copy, 0, 1, 0, 0, quarter)
            if i == 6:
                prepare(s_copy, 0, 1, 0, quarter, quarter)
        nc.vector.tensor_copy(
            out=norm_cols[:, 0:CHUNKS], in_=gain_bf[:].rearrange("p g t -> p (g t)")
        )
        aggregate(7)
        nc.vector.tensor_copy(
            out=norm_cols[:, CHUNKS : 2 * CHUNKS], in_=lnb_bf[:].rearrange("p g t -> p (g t)")
        )
        for j in range(CHUNKS):
            scale_and_shift(0, j, transpose(0, j))
            if j == 0:
                deviation(7)
        normalise(nc.vector, shift_v, 6)
        normalise(nc.vector, shift_v, 7)
        prepare(v_copy, 0, 0, 1)
        h00 = regroup_h(0, 0)
        quantise_piece(0, 0, 0)
        quantise_h(0, 0, h00)
        h01 = regroup_h(0, 1)
        quantise_piece(0, 0, 1)
        quantise_h(0, 1, h01)
        for j in range(CHUNKS):
            scale_and_shift(1, j, transpose(1, j))
        h11 = h_stage.tile([P, HALF_TOKENS, PACK], BF16, align_bytes=64)
        regroup(s_copy, h11[:], h_rows[:, 1, PACK : 2 * PACK, :])
        prepare(s_copy, 0, 1, 1)
        prepare(s_copy, 1, 0, 0)
        prepare(s_copy, 1, 0, 1)
        h10 = regroup_h(1, 0)
        for i in range(4):
            store(*project(0, 0, i))
        quantise_h(1, 0, h10)
        quantise_piece(0, 1, 0)
        quantise_h(1, 1, h11)
        for i in range(4, 8):
            store(*project(0, 0, i))
            if i == 5:
                quantise_piece(0, 1, 1)
        order = [(w, part) for w in range(WEIGHTS) for part in range(PARTS)]
        pieces = [(w, part, g) for w, part in order[1:] for g in range(PASSES)]
        prepared, quantised = 4, 2
        for n in range(1, len(order)):
            for i in range(TOKEN_TILES):
                if i in (0, 4) and prepared < len(pieces):
                    prepare(s_copy, *pieces[prepared])
                    prepared += 1
                store(*project(*order[n], i))
                if i in (0, 3) and quantised < len(pieces):
                    quantise_piece(*pieces[quantised])
                    quantised += 1
